import numpy as np
import ml_dtypes


def mxq(x, axis, fmt="e4m3"):
    dtype, down = {"e4m3": (ml_dtypes.float8_e4m3fn, 7), "e5m2": (ml_dtypes.float8_e5m2, 14)}[fmt]
    v = np.moveaxis(np.asarray(x, np.float32).astype(ml_dtypes.bfloat16).astype(np.float64), axis, -1)
    blocks = v.reshape(v.shape[:-1] + (-1, 32))
    amax = np.abs(blocks).max(-1, keepdims=True)
    byte = np.maximum(np.where(amax > 0, np.frexp(amax)[1] - 1 + 127, 0) - down, 1)
    scale = np.exp2(byte - 127.0)
    codes = (blocks / scale).astype(np.float32).astype(dtype).astype(np.float64)
    return np.moveaxis((codes * scale).reshape(v.shape), -1, axis)


WIDE = False


def mx_kscale(k):
    if not WIDE:
        return np.ones(k)
    levels = np.array([10, -10, 5, -5, 0])
    a = np.random.permutation(np.resize(levels, k // 512 * 4)).reshape(k // 512, 4)
    idx = np.arange(k)
    return np.exp2(a[idx // 512, idx % 128 // 32])


BF16 = ml_dtypes.bfloat16


def bf(x):
    return np.asarray(x, np.float32).astype(BF16)


def f64(x):
    return np.asarray(x).astype(np.float64)


E2M1 = np.array([0.0, 0.5, 1.0, 1.5, 2.0, 3.0, 4.0, 6.0, -0.0, -0.5, -1.0, -1.5, -2.0, -3.0, -4.0, -6.0])


def pack_weight(w, fmt):
    k, n = w.shape
    w = f64(bf(w)).reshape(k // 32, 32, n)
    amax = np.abs(w).max(1)
    if fmt == "e4m3":
        byte = np.frexp(amax)[1] - 1 + 127 - 7
    else:
        mant, ex = np.frexp(amax / 6.0)
        byte = np.where(mant > 0.5, ex, ex - 1) + 127
    byte = np.clip(np.where(amax > 0, byte, 1), 1, 254)
    scaled = (w * np.exp2(127.0 - byte)[:, None, :]).reshape(k, n).astype(np.float32)
    by_word = np.ascontiguousarray(scaled.reshape(k // 512, 128, 4, n).transpose(0, 1, 3, 2))
    if fmt == "e4m3":
        words = by_word.astype(ml_dtypes.float8_e4m3fn).view(np.uint8)
    else:
        c = by_word.astype(ml_dtypes.float4_e2m1fn).view(np.uint8) & 0xF
        words = c[..., 0::2] | (c[..., 1::2] << 4)
    return np.ascontiguousarray(words), np.ascontiguousarray(byte.astype(np.uint8).reshape(k // 512, 16, n))


def unpack_weight(words, scales, fmt):
    g, p, n, _ = words.shape
    if fmt == "e4m3":
        vals = np.ascontiguousarray(words).view(ml_dtypes.float8_e4m3fn).astype(np.float64)
    else:
        nib = np.empty((g, p, n, 4), np.uint8)
        nib[..., 0::2] = words & 0xF
        nib[..., 1::2] = words >> 4
        vals = E2M1[nib]
    vals = vals * np.repeat(np.exp2(scales.astype(np.float64) - 127.0), 8, axis=1)[..., None]
    return vals.transpose(0, 1, 3, 2).reshape(g * 512, n)


B, C, H, W, K, O = 2, 512, 8, 8, 3, 4096
P = C * K * K
PAD = 1
G = 32
FMT = "e4m3"


def im2col(a):
    a_pad = np.pad(a, ((0, 0), (0, 0), (PAD, PAD), (PAD, PAD)), mode="reflect")
    cols = np.stack([a_pad[:, :, kh:kh + H, kw:kw + W] for kh in range(K) for kw in range(K)], axis=2)
    cols = cols.reshape(B, P, H * W)
    return np.swapaxes(cols, 1, 2)


def setup_inputs():
    u = np.unique(mx_kscale(P))
    t = u[np.arange(C // G) % len(u)]
    sc = np.repeat(t, G).reshape(1, C, 1, 1)
    sp = np.repeat(t, G * K * K).reshape(P, 1)
    lam = 1.0 if len(u) == 1 else 0.0
    g = 2.0 ** np.round(0.5 * np.log2(np.mean(t ** 2)))
    amp = 0.5 + 1.5 * np.random.random_sample((B, 1, H, W))
    off = 0.6 + 0.4 * np.random.standard_normal((B, 1, H, W))
    bound = np.sqrt(6.0 / P)
    z = np.random.standard_normal((B, C, H, W))
    z[:, 1::2] = lam * z[:, 1::2] - (1.0 - lam) * z[:, 0::2]
    a = bf((z * amp + off * lam) * sc)
    words, scales = pack_weight(np.random.uniform(-bound, bound, (P, O)) * g / sp, FMT)
    return {"a": a,
            "conv_kernel_words": words,
            "conv_kernel_scales": scales}


def reference(a, conv_kernel_words, conv_kernel_scales):
    patches = im2col(f64(a))
    mean = np.mean(patches, axis=-1, keepdims=True)
    std = np.std(patches, axis=-1, keepdims=True, ddof=1)
    normed = (patches - mean) / std
    out = mxq(normed, 2, "e4m3") @ unpack_weight(conv_kernel_words, conv_kernel_scales, FMT)
    return np.swapaxes(out, 1, 2).reshape(B, O, H, W)

@@ -1,0 +1,224 @@
+from contextlib import ExitStack
+
+import concourse.mybir as mybir
+from concourse.masks import make_identity
+
+F32 = mybir.dt.float32
+BF16 = mybir.dt.bfloat16
+I32 = mybir.dt.int32
+U8 = mybir.dt.uint8
+FP8X4 = mybir.dt.float8_e4m3fn_x4
+ALU = mybir.AluOpType
+ACT = mybir.ActivationFunctionType
+
+P = 128
+TAPS = 9
+CHANNELS = 512
+PATCH = CHANNELS * TAPS
+PASSES = PATCH // 512
+OUTS = 4096
+BANK = 512
+HALF = 2048
+FLOPS = 2 * P * PATCH * OUTS
+
+
+def tile_norm_conv_w_kernel(tc, a, conv_kernel_words, conv_kernel_scales, out):
+    nc = tc.nc
+    with ExitStack() as ctx:
+        ctx.enter_context(tc.manual_schedule())
+        keep = ctx.enter_context(tc.tile_pool(name="keep", bufs=1))
+        psum = ctx.enter_context(tc.psum_pool(name="psum", bufs=1))
+
+        def bank(i, shape, dtype, name):
+            return psum.tile(shape, dtype, tag="bank%d" % i, name=name)
+
+        ident_bf = keep.tile([P, P], BF16, name="ident_bf")
+        make_identity(nc, ident_bf[:])
+        ident_f = keep.tile([P, P], F32, name="ident_f")
+        make_identity(nc, ident_f[:])
+        planes = keep.tile([P, 2 * OUTS + 1024], U8, name="planes", align_bytes=64)
+        planes32 = planes[:].bitcast(I32)
+        nc.vector.memset(planes32, 0)
+
+        a_sb = keep.tile([P, 4, 2, 64], BF16, name="a_sb")
+        for b in range(2):
+            nc.sync.dma_start(out=a_sb[:, :, b, :], in_=a[b].rearrange("(p h) i j -> p h (i j)", h=4))
+        sc32 = conv_kernel_scales.bitcast(I32)
+        for s in range(2):
+            for q in (0, 2, 1, 3):
+                nc.sync.dma_start(
+                    out=planes32[32 * q : 32 * q + 16, 1024 * s : 1024 * (s + 1)],
+                    in_=sc32[4 * s : 4 * s + 4, 4 * q : 4 * q + 4, :],
+                )
+        for q in (0, 2, 1, 3):
+            nc.sync.dma_start(
+                out=planes32[32 * q : 32 * q + 16, 2048:2304],
+                in_=sc32[8, 4 * q : 4 * q + 4, :].rearrange("r (k c) -> k r c", k=4),
+            )
+        w32 = conv_kernel_words.rearrange("g p n t -> g p (n t)").bitcast(I32)
+        w_piece = {}
+        for blk in range(2):
+            for g in range(PASSES):
+                if blk == 1 and g == PASSES - 1:
+                    for beta in range(4):
+                        wt = keep.tile([P, BANK], I32, name="w_last_%d" % beta, align_bytes=64)
+                        n0 = HALF + BANK * beta
+                        nc.sync.dma_start(out=wt[:], in_=w32[g, :, n0 : n0 + BANK])
+                        w_piece[(blk, g, beta)] = wt[:]
+                else:
+                    wt = keep.tile([P, HALF], I32, name="w_%d_%d" % (blk, g), align_bytes=64)
+                    nc.sync.dma_start(out=wt[:], in_=w32[g, :, HALF * blk : HALF * (blk + 1)])
+                    for beta in range(4):
+                        w_piece[(blk, g, beta)] = wt[:, BANK * beta : BANK * (beta + 1)]
+
+        def plane_of(g, n0):
+            if g < 8:
+                k = g % 4
+                c0 = OUTS * (g // 4) + n0
+            else:
+                k = n0 // 1024
+                c0 = 2 * OUTS + n0 % 1024
+            return planes[4 * k : P, c0 : c0 + BANK]
+
+        ipad = keep.tile([P, 2, 10, 10], BF16, name="ipad")
+        ident4 = ident_bf[:].rearrange("p (b i j) -> p b i j", b=2, i=8)
+        nc.vector.tensor_copy(out=ipad[:, :, 1:9, 1:9], in_=ident4)
+        nc.vector.tensor_copy(out=ipad[:, :, 0, 1:9], in_=ident4[:, :, 1, :])
+        nc.vector.tensor_copy(out=ipad[:, :, 9, 1:9], in_=ident4[:, :, 6, :])
+        nc.vector.tensor_copy(out=ipad[:, :, :, 0], in_=ipad[:, :, :, 2])
+        nc.vector.tensor_copy(out=ipad[:, :, :, 9], in_=ipad[:, :, :, 7])
+        sel = keep.tile([P, TAPS, P], BF16, name="sel")
+        for kh in range(3):
+            for kw in range(3):
+                nc.vector.tensor_copy(
+                    out=sel[:, 3 * kh + kw, :].rearrange("p (b i j) -> p b i j", b=2, i=8),
+                    in_=ipad[:, :, kh : kh + 8, kw : kw + 8],
+                )
+
+        at_ps = bank(7, [P, 4, P], BF16, "at_ps")
+        for h in range(4):
+            nc.tensor.transpose(at_ps[:, h, :], a_sb[:, h, :, :].rearrange("p b x -> p (b x)"), ident_bf[:])
+        at_sb = keep.tile([P, CHANNELS], BF16, name="at_sb")
+        nc.vector.tensor_copy(
+            out=at_sb[:].rearrange("q (p h) -> q p h", h=4), in_=at_ps[:].rearrange("q h p -> q p h")
+        )
+
+        ptap = keep.tile([P, TAPS, CHANNELS], BF16, name="ptap")
+        stats = keep.tile([P, TAPS, 6], F32, name="stats")
+        sums = keep.tile([P, TAPS], F32, name="sums")
+        for tap in range(TAPS):
+            pt = bank(tap % 8, [P, CHANNELS], F32, "pt_%d" % tap)
+            nc.tensor.matmul(pt[:], lhsT=sel[:, tap, :], rhs=at_sb[:], start=True, stop=True)
+            nc.scalar.activation(out=ptap[:, tap, :], in_=pt[:], func=ACT.Copy, accum_out=sums[:, tap : tap + 1])
+            nc.vector.bn_stats(out=stats[:, tap, :], in_=ptap[:, tap, :])
+        mv = keep.tile([P, 2], F32, name="mv")
+        nc.vector.bn_aggr(out=mv[:], in_=stats[:].rearrange("p t s -> p (t s)"))
+        total = keep.tile([P, 1], F32, name="total")
+        nc.vector.tensor_reduce(out=total[:], in_=sums[:], axis=mybir.AxisListType.X, op=ALU.add)
+        mean = keep.tile([P, 1], F32, name="mean")
+        nc.vector.tensor_scalar(out=mean[:], in0=total[:], scalar1=1.0 / PATCH, scalar2=None, op0=ALU.mult)
+        std = keep.tile([P, 1], F32, name="std")
+        nc.scalar.activation(out=std[:], in_=mv[:, 1:2], func=ACT.Sqrt, scale=PATCH / (PATCH - 1.0))
+        rstd = keep.tile([P, 1], F32, name="rstd")
+        nc.vector.reciprocal(out=rstd[:], in_=std[:])
+        nmr = keep.tile([P, 1], F32, name="nmr")
+        nc.vector.tensor_scalar(
+            out=nmr[:], in0=mean[:, 0:1], scalar1=rstd[:, 0:1], scalar2=-1.0, op0=ALU.mult, op1=ALU.mult
+        )
+
+        pn = keep.tile([P, PATCH], BF16, name="pn")
+        for j in range(8):
+            dst = pn[:, 576 * j : 576 * (j + 1)].rearrange("p (c t) -> p c t", t=TAPS)
+            src = ptap[:, :, 64 * j : 64 * (j + 1)].rearrange("p t c -> p c t")
+            if j in (2, 5, 7):
+                nc.scalar.activation(out=dst, in_=src, func=ACT.Identity, scale=rstd[:, 0:1], bias=nmr[:, 0:1])
+            else:
+                nc.vector.tensor_scalar(
+                    out=dst, in0=src, scalar1=mean[:, 0:1], scalar2=rstd[:, 0:1], op0=ALU.subtract, op1=ALU.mult
+                )
+
+        grouped = keep.tile([P, PASSES, 4 * P], BF16, name="grouped", align_bytes=64)
+        xc = keep.tile([P, PASSES, P], I32, name="xc", align_bytes=64)
+        xs = keep.tile([P, PASSES, P], U8, name="xs", align_bytes=64)
+
+        def quantise(g):
+            nc.vector.quantize_mx(out=xc[:, g, :].bitcast(FP8X4), scales=xs[:, g, :], in_=grouped[:, g, :])
+
+        for g in range(PASSES):
+            xt = bank((g + 1) % 8, [P, 4, P], BF16, "xt_%d" % g)
+            for t in range(4):
+                nc.tensor.transpose(xt[:, t, :], pn[:, 512 * g + t : 512 * (g + 1) : 4], ident_bf[:])
+            dst = grouped[:, g, :].rearrange("p (r t) -> p r t", t=4)
+            src = xt[:].rearrange("p t r -> p r t")
+            if g % 2 == 0:
+                nc.vector.tensor_copy(out=dst, in_=src)
+            else:
+                nc.scalar.copy(out=dst, in_=src)
+            if g >= 1:
+                quantise(g - 1)
+        quantise(PASSES - 1)
+
+        acc = {}
+
+        def passes(blk, g):
+            for beta in range(4):
+                if g == 0:
+                    acc[(blk, beta)] = bank(4 * blk + beta, [P, BANK], F32, "acc_%d_%d" % (blk, beta))
+                nc.tensor.matmul_mx(
+                    out=acc[(blk, beta)][:],
+                    lhsT=xc[:, g, :].bitcast(FP8X4),
+                    lhsT_scale=xs[:, g, :],
+                    rhs=w_piece[(blk, g, beta)].bitcast(FP8X4),
+                    rhs_scale=plane_of(g, HALF * blk + BANK * beta),
+                    start=(g == 0),
+                    stop=(g == PASSES - 1),
+                )
+
+        def copy_on(which, dst, src):
+            if which % 2 == 0:
+                nc.vector.tensor_copy(out=dst, in_=src)
+            else:
+                nc.scalar.copy(out=dst, in_=src)
+
+        def sort_out(banks, per, r_sb, first):
+            width = BANK // per
+            for i, bk in enumerate(banks):
+                copy_on(
+                    first + i,
+                    r_sb[:, :, width * i : width * (i + 1)],
+                    bk[:].rearrange("t (p j) -> t j p", j=per),
+                )
+
+        def flip_and_store(n0, per, r_sb, o_sb, first, label):
+            for jj in range(per // 4):
+                tp = bank((first + jj) % 4, [P, 4, P], F32, "tp_%s_%d" % (label, jj))
+                for j in range(4):
+                    nc.tensor.transpose(tp[:, j, :], r_sb[:, 4 * jj + j, :], ident_f[:])
+                copy_on(
+                    first + jj,
+                    o_sb[:, :, 4 * jj : 4 * jj + 4, :],
+                    tp[:].rearrange("p j (b x) -> p b j x", b=2),
+                )
+            nc.sync.dma_start(
+                out=out[:, n0 : n0 + P * per].rearrange("b (p j) i x -> p b (j i x)", j=per),
+                in_=o_sb[:].rearrange("p b j x -> p b (j x)"),
+            )
+
+        for g in range(PASSES):
+            passes(0, g)
+        r0 = keep.tile([P, 16, P], F32, name="r0")
+        o0 = keep.tile([P, 2, 16, 64], F32, name="o0")
+        sort_out([acc[(0, beta)] for beta in range(4)], 16, r0, 0)
+        passes(1, 0)
+        passes(1, 1)
+        flip_and_store(0, 16, r0, o0, 0, "a")
+        for g in range(2, PASSES):
+            passes(1, g)
+        r1 = []
+        o1 = []
+        for beta in range(4):
+            r1.append(keep.tile([P, 4, P], F32, name="r1_%d" % beta))
+            o1.append(keep.tile([P, 2, 4, 64], F32, name="o1_%d" % beta))
+            sort_out([acc[(1, beta)]], 4, r1[beta], beta)
+        for beta in range(4):
+            flip_and_store(HALF + BANK * beta, 4, r1[beta], o1[beta], beta, "b%d" % beta)

@@ -43,16 +43,17 @@ def tile_norm_conv_w_kernel(tc, a, conv_kernel_words, conv_kernel_scales, out):
         a_sb = keep.tile([P, 4, 2, 64], BF16, name="a_sb")
         for b in range(2):
             nc.sync.dma_start(out=a_sb[:, :, b, :], in_=a[b].rearrange("(p h) i j -> p h (i j)", h=4))
-        sc32 = conv_kernel_scales.bitcast(I32)
+        sc32 = conv_kernel_scales.bitcast(F32)
+        planes_f = planes[:].bitcast(F32)
         for s in range(2):
             for q in (0, 2, 1, 3):
-                nc.sync.dma_start(
-                    out=planes32[32 * q : 32 * q + 16, 1024 * s : 1024 * (s + 1)],
+                nc.gpsimd.dma_start(
+                    out=planes_f[32 * q : 32 * q + 16, 1024 * s : 1024 * (s + 1)],
                     in_=sc32[4 * s : 4 * s + 4, 4 * q : 4 * q + 4, :],
                 )
         for q in (0, 2, 1, 3):
-            nc.sync.dma_start(
-                out=planes32[32 * q : 32 * q + 16, 2048:2304],
+            nc.gpsimd.dma_start(
+                out=planes_f[32 * q : 32 * q + 16, 2048:2304],
                 in_=sc32[8, 4 * q : 4 * q + 4, :].rearrange("r (k c) -> k r c", k=4),
             )
         w32 = conv_kernel_words.rearrange("g p n t -> g p (n t)").bitcast(I32)

@@ -36,6 +36,10 @@ def tile_norm_conv_w_kernel(tc, a, conv_kernel_words, conv_kernel_scales, out):
         make_identity(nc, ident_bf[:])
         ident_f = keep.tile([P, P], F32, name="ident_f")
         make_identity(nc, ident_f[:])
+        one = keep.tile([P, 1], F32, name="one")
+        nc.gpsimd.memset(one[:], 1.0)
+        warm = keep.tile([P, 1], F32, name="warm")
+        nc.scalar.activation(out=warm[:], in_=one[:], func=ACT.Sqrt)
         planes = keep.tile([P, 2 * OUTS + 1024], U8, name="planes", align_bytes=64)
         planes32 = planes[:].bitcast(I32)
         nc.vector.memset(planes32, 0)
@@ -43,17 +47,16 @@ def tile_norm_conv_w_kernel(tc, a, conv_kernel_words, conv_kernel_scales, out):
         a_sb = keep.tile([P, 4, 2, 64], BF16, name="a_sb")
         for b in range(2):
             nc.sync.dma_start(out=a_sb[:, :, b, :], in_=a[b].rearrange("(p h) i j -> p h (i j)", h=4))
-        sc32 = conv_kernel_scales.bitcast(F32)
-        planes_f = planes[:].bitcast(F32)
+        sc32 = conv_kernel_scales.bitcast(I32)
         for s in range(2):
             for q in (0, 2, 1, 3):
-                nc.gpsimd.dma_start(
-                    out=planes_f[32 * q : 32 * q + 16, 1024 * s : 1024 * (s + 1)],
+                nc.sync.dma_start(
+                    out=planes32[32 * q : 32 * q + 16, 1024 * s : 1024 * (s + 1)],
                     in_=sc32[4 * s : 4 * s + 4, 4 * q : 4 * q + 4, :],
                 )
         for q in (0, 2, 1, 3):
-            nc.gpsimd.dma_start(
-                out=planes_f[32 * q : 32 * q + 16, 2048:2304],
+            nc.sync.dma_start(
+                out=planes32[32 * q : 32 * q + 16, 2048:2304],
                 in_=sc32[8, 4 * q : 4 * q + 4, :].rearrange("r (k c) -> k r c", k=4),
             )
         w32 = conv_kernel_words.rearrange("g p n t -> g p (n t)").bitcast(I32)
@@ -106,20 +109,27 @@ def tile_norm_conv_w_kernel(tc, a, conv_kernel_words, conv_kernel_scales, out):
 
         ptap = keep.tile([P, TAPS, CHANNELS], BF16, name="ptap")
         stats = keep.tile([P, TAPS, 6], F32, name="stats")
-        sums = keep.tile([P, TAPS], F32, name="sums")
-        for tap in range(TAPS):
-            pt = bank(tap % 8, [P, CHANNELS], F32, "pt_%d" % tap)
-            nc.tensor.matmul(pt[:], lhsT=sel[:, tap, :], rhs=at_sb[:], start=True, stop=True)
-            nc.scalar.activation(out=ptap[:, tap, :], in_=pt[:], func=ACT.Copy, accum_out=sums[:, tap : tap + 1])
-            nc.vector.bn_stats(out=stats[:, tap, :], in_=ptap[:, tap, :])
+        for pair in range(5):
+            taps = [tap for tap in (2 * pair, 2 * pair + 1) if tap < TAPS]
+            pt = bank(pair, [P, 2, CHANNELS], BF16, "pt_%d" % pair)
+            for i, tap in enumerate(taps):
+                nc.tensor.matmul(pt[:, i, :], lhsT=sel[:, tap, :], rhs=at_sb[:], start=True, stop=True)
+            for i, tap in enumerate(taps):
+                nc.vector.bn_stats(out=stats[:, tap, :], in_=pt[:, i, :])
+            nc.scalar.copy(out=ptap[:, taps[0] : taps[0] + len(taps), :], in_=pt[:, 0 : len(taps), :])
         mv = keep.tile([P, 2], F32, name="mv")
         nc.vector.bn_aggr(out=mv[:], in_=stats[:].rearrange("p t s -> p (t s)"))
-        total = keep.tile([P, 1], F32, name="total")
-        nc.vector.tensor_reduce(out=total[:], in_=sums[:], axis=mybir.AxisListType.X, op=ALU.add)
-        mean = keep.tile([P, 1], F32, name="mean")
-        nc.vector.tensor_scalar(out=mean[:], in0=total[:], scalar1=1.0 / PATCH, scalar2=None, op0=ALU.mult)
         std = keep.tile([P, 1], F32, name="std")
         nc.scalar.activation(out=std[:], in_=mv[:, 1:2], func=ACT.Sqrt, scale=PATCH / (PATCH - 1.0))
+        total = keep.tile([P, 1], F32, name="total")
+        nc.vector.tensor_reduce(
+            out=total[:],
+            in_=stats[:].rearrange("p t (e s) -> p (t e) s", s=3)[:, :, 1],
+            axis=mybir.AxisListType.X,
+            op=ALU.add,
+        )
+        mean = keep.tile([P, 1], F32, name="mean")
+        nc.vector.tensor_scalar(out=mean[:], in0=total[:], scalar1=1.0 / (2 * TAPS), scalar2=None, op0=ALU.mult)
         rstd = keep.tile([P, 1], F32, name="rstd")
         nc.vector.reciprocal(out=rstd[:], in_=std[:])
         nmr = keep.tile([P, 1], F32, name="nmr")
@@ -128,36 +138,33 @@ def tile_norm_conv_w_kernel(tc, a, conv_kernel_words, conv_kernel_scales, out):
         )
 
         pn = keep.tile([P, PATCH], BF16, name="pn")
-        for j in range(8):
+        grouped = keep.tile([P, PASSES, 4 * P], BF16, name="grouped", align_bytes=64)
+        xc = keep.tile([P, PASSES, P], I32, name="xc", align_bytes=64)
+        xs = keep.tile([P, PASSES, P], U8, name="xs", align_bytes=64)
+
+        def normalise(j):
             dst = pn[:, 576 * j : 576 * (j + 1)].rearrange("p (c t) -> p c t", t=TAPS)
             src = ptap[:, :, 64 * j : 64 * (j + 1)].rearrange("p t c -> p c t")
-            if j in (2, 5, 7):
+            if j % 2 == 1:
                 nc.scalar.activation(out=dst, in_=src, func=ACT.Identity, scale=rstd[:, 0:1], bias=nmr[:, 0:1])
             else:
                 nc.vector.tensor_scalar(
                     out=dst, in0=src, scalar1=mean[:, 0:1], scalar2=rstd[:, 0:1], op0=ALU.subtract, op1=ALU.mult
                 )
 
-        grouped = keep.tile([P, PASSES, 4 * P], BF16, name="grouped", align_bytes=64)
-        xc = keep.tile([P, PASSES, P], I32, name="xc", align_bytes=64)
-        xs = keep.tile([P, PASSES, P], U8, name="xs", align_bytes=64)
-
-        def quantise(g):
-            nc.vector.quantize_mx(out=xc[:, g, :].bitcast(FP8X4), scales=xs[:, g, :], in_=grouped[:, g, :])
-
-        for g in range(PASSES):
-            xt = bank((g + 1) % 8, [P, 4, P], BF16, "xt_%d" % g)
+        def flip(g):
+            xt = bank(4 + g % 4, [P, 4, P], BF16, "xt_%d" % g)
             for t in range(4):
                 nc.tensor.transpose(xt[:, t, :], pn[:, 512 * g + t : 512 * (g + 1) : 4], ident_bf[:])
             dst = grouped[:, g, :].rearrange("p (r t) -> p r t", t=4)
             src = xt[:].rearrange("p t r -> p r t")
-            if g % 2 == 0:
+            if g % 3 == 2:
                 nc.vector.tensor_copy(out=dst, in_=src)
             else:
                 nc.scalar.copy(out=dst, in_=src)
-            if g >= 1:
-                quantise(g - 1)
-        quantise(PASSES - 1)
+
+        def quantise(g):
+            nc.vector.quantize_mx(out=xc[:, g, :].bitcast(FP8X4), scales=xs[:, g, :], in_=grouped[:, g, :])
 
         acc = {}
 
@@ -205,8 +212,14 @@ def tile_norm_conv_w_kernel(tc, a, conv_kernel_words, conv_kernel_scales, out):
                 in_=o_sb[:].rearrange("p b j x -> p b (j x)"),
             )
 
-        for g in range(PASSES):
-            passes(0, g)
+        for step in range(PASSES + 2):
+            if step < 8:
+                normalise(step)
+            if 1 <= step <= PASSES:
+                flip(step - 1)
+            if step >= 2:
+                quantise(step - 2)
+                passes(0, step - 2)
         r0 = keep.tile([P, 16, P], F32, name="r0")
         o0 = keep.tile([P, 2, 16, 64], F32, name="o0")
         sort_out([acc[(0, beta)] for beta in range(4)], 16, r0, 0)

@@ -34,8 +34,6 @@ def tile_norm_conv_w_kernel(tc, a, conv_kernel_words, conv_kernel_scales, out):
 
         ident_bf = keep.tile([P, P], BF16, name="ident_bf")
         make_identity(nc, ident_bf[:])
-        ident_f = keep.tile([P, P], F32, name="ident_f")
-        make_identity(nc, ident_f[:])
         one = keep.tile([P, 1], F32, name="one")
         nc.gpsimd.memset(one[:], 1.0)
         warm = keep.tile([P, 1], F32, name="warm")
@@ -47,18 +45,21 @@ def tile_norm_conv_w_kernel(tc, a, conv_kernel_words, conv_kernel_scales, out):
         a_sb = keep.tile([P, 4, 2, 64], BF16, name="a_sb")
         for b in range(2):
             nc.sync.dma_start(out=a_sb[:, :, b, :], in_=a[b].rearrange("(p h) i j -> p h (i j)", h=4))
-        sc32 = conv_kernel_scales.bitcast(I32)
+        sc32 = conv_kernel_scales.bitcast(F32)
+        planes_f = planes[:].bitcast(F32)
         for s in range(2):
             for q in (0, 2, 1, 3):
-                nc.sync.dma_start(
-                    out=planes32[32 * q : 32 * q + 16, 1024 * s : 1024 * (s + 1)],
+                nc.gpsimd.dma_start(
+                    out=planes_f[32 * q : 32 * q + 16, 1024 * s : 1024 * (s + 1)],
                     in_=sc32[4 * s : 4 * s + 4, 4 * q : 4 * q + 4, :],
                 )
         for q in (0, 2, 1, 3):
-            nc.sync.dma_start(
-                out=planes32[32 * q : 32 * q + 16, 2048:2304],
+            nc.gpsimd.dma_start(
+                out=planes_f[32 * q : 32 * q + 16, 2048:2304],
                 in_=sc32[8, 4 * q : 4 * q + 4, :].rearrange("r (k c) -> k r c", k=4),
             )
+        ident_f = keep.tile([P, P], F32, name="ident_f")
+        make_identity(nc, ident_f[:])
         w32 = conv_kernel_words.rearrange("g p n t -> g p (n t)").bitcast(I32)
         w_piece = {}
         for blk in range(2):

@@ -34,28 +34,35 @@ def tile_norm_conv_w_kernel(tc, a, conv_kernel_words, conv_kernel_scales, out):
 
         ident_bf = keep.tile([P, P], BF16, name="ident_bf")
         make_identity(nc, ident_bf[:])
-        one = keep.tile([P, 1], F32, name="one")
-        nc.gpsimd.memset(one[:], 1.0)
-        warm = keep.tile([P, 1], F32, name="warm")
-        nc.scalar.activation(out=warm[:], in_=one[:], func=ACT.Sqrt)
         planes = keep.tile([P, 2 * OUTS + 1024], U8, name="planes", align_bytes=64)
         planes32 = planes[:].bitcast(I32)
-        nc.vector.memset(planes32, 0)
+        planes_f = planes[:].bitcast(F32)
+        for lo, hi in ((0, 1024), (1024, 2048), (2048, 2304)):
+            nc.vector.memset(planes32[:, lo:hi], 0)
+        one = keep.tile([P, 1], F32, name="one")
+        nc.vector.memset(one[:], 1.0)
+        warm = keep.tile([P, 1], F32, name="warm")
+        nc.scalar.activation(out=warm[:], in_=one[:], func=ACT.Sqrt)
 
         a_sb = keep.tile([P, 4, 2, 64], BF16, name="a_sb")
         for b in range(2):
             nc.sync.dma_start(out=a_sb[:, :, b, :], in_=a[b].rearrange("(p h) i j -> p h (i j)", h=4))
-        sc32 = conv_kernel_scales.bitcast(F32)
-        planes_f = planes[:].bitcast(F32)
+        sc32 = conv_kernel_scales.bitcast(I32)
+        sc_f = conv_kernel_scales.bitcast(F32)
         for s in range(2):
-            for q in (0, 2, 1, 3):
-                nc.gpsimd.dma_start(
-                    out=planes_f[32 * q : 32 * q + 16, 1024 * s : 1024 * (s + 1)],
+            for q in (0, 1):
+                nc.sync.dma_start(
+                    out=planes32[32 * q : 32 * q + 16, 1024 * s : 1024 * (s + 1)],
                     in_=sc32[4 * s : 4 * s + 4, 4 * q : 4 * q + 4, :],
                 )
+            for q in (2, 3):
+                nc.gpsimd.dma_start(
+                    out=planes_f[32 * q : 32 * q + 16, 1024 * s : 1024 * (s + 1)],
+                    in_=sc_f[4 * s : 4 * s + 4, 4 * q : 4 * q + 4, :],
+                )
         for q in (0, 2, 1, 3):
-            nc.gpsimd.dma_start(
-                out=planes_f[32 * q : 32 * q + 16, 2048:2304],
+            nc.sync.dma_start(
+                out=planes32[32 * q : 32 * q + 16, 2048:2304],
                 in_=sc32[8, 4 * q : 4 * q + 4, :].rearrange("r (k c) -> k r c", k=4),
             )
         ident_f = keep.tile([P, P], F32, name="ident_f")

from contextlib import ExitStack

import concourse.mybir as mybir
from concourse.masks import make_identity

F32 = mybir.dt.float32
BF16 = mybir.dt.bfloat16
I32 = mybir.dt.int32
U8 = mybir.dt.uint8
FP8X4 = mybir.dt.float8_e4m3fn_x4
ALU = mybir.AluOpType
ACT = mybir.ActivationFunctionType

P = 128
TAPS = 9
CHANNELS = 512
PATCH = CHANNELS * TAPS
PASSES = PATCH // 512
OUTS = 4096
BANK = 512
HALF = 2048
FLOPS = 2 * P * PATCH * OUTS


def tile_norm_conv_w_kernel(tc, a, conv_kernel_words, conv_kernel_scales, out):
    nc = tc.nc
    with ExitStack() as ctx:
        ctx.enter_context(tc.manual_schedule())
        keep = ctx.enter_context(tc.tile_pool(name="keep", bufs=1))
        psum = ctx.enter_context(tc.psum_pool(name="psum", bufs=1))

        def bank(i, shape, dtype, name):
            return psum.tile(shape, dtype, tag="bank%d" % i, name=name)

        ident_bf = keep.tile([P, P], BF16, name="ident_bf")
        make_identity(nc, ident_bf[:])
        planes = keep.tile([P, 2 * OUTS + 1024], U8, name="planes", align_bytes=64)
        planes32 = planes[:].bitcast(I32)
        planes_f = planes[:].bitcast(F32)
        for lo, hi in ((0, 1024), (1024, 2048), (2048, 2304)):
            nc.vector.memset(planes32[:, lo:hi], 0)
        one = keep.tile([P, 1], F32, name="one")
        nc.vector.memset(one[:], 1.0)
        warm = keep.tile([P, 1], F32, name="warm")
        nc.scalar.activation(out=warm[:], in_=one[:], func=ACT.Sqrt)

        a_sb = keep.tile([P, 4, 2, 64], BF16, name="a_sb")
        for b in range(2):
            nc.sync.dma_start(out=a_sb[:, :, b, :], in_=a[b].rearrange("(p h) i j -> p h (i j)", h=4))
        sc32 = conv_kernel_scales.bitcast(I32)
        sc_f = conv_kernel_scales.bitcast(F32)
        for s in range(2):
            for q in (0, 1):
                nc.sync.dma_start(
                    out=planes32[32 * q : 32 * q + 16, 1024 * s : 1024 * (s + 1)],
                    in_=sc32[4 * s : 4 * s + 4, 4 * q : 4 * q + 4, :],
                )
            for q in (2, 3):
                nc.gpsimd.dma_start(
                    out=planes_f[32 * q : 32 * q + 16, 1024 * s : 1024 * (s + 1)],
                    in_=sc_f[4 * s : 4 * s + 4, 4 * q : 4 * q + 4, :],
                )
        for q in (0, 2, 1, 3):
            nc.sync.dma_start(
                out=planes32[32 * q : 32 * q + 16, 2048:2304],
                in_=sc32[8, 4 * q : 4 * q + 4, :].rearrange("r (k c) -> k r c", k=4),
            )
        ident_f = keep.tile([P, P], F32, name="ident_f")
        make_identity(nc, ident_f[:])
        w32 = conv_kernel_words.rearrange("g p n t -> g p (n t)").bitcast(I32)
        w_piece = {}
        for blk in range(2):
            for g in range(PASSES):
                if blk == 1 and g == PASSES - 1:
                    for beta in range(4):
                        wt = keep.tile([P, BANK], I32, name="w_last_%d" % beta, align_bytes=64)
                        n0 = HALF + BANK * beta
                        nc.sync.dma_start(out=wt[:], in_=w32[g, :, n0 : n0 + BANK])
                        w_piece[(blk, g, beta)] = wt[:]
                else:
                    wt = keep.tile([P, HALF], I32, name="w_%d_%d" % (blk, g), align_bytes=64)
                    nc.sync.dma_start(out=wt[:], in_=w32[g, :, HALF * blk : HALF * (blk + 1)])
                    for beta in range(4):
                        w_piece[(blk, g, beta)] = wt[:, BANK * beta : BANK * (beta + 1)]

        def plane_of(g, n0):
            if g < 8:
                k = g % 4
                c0 = OUTS * (g // 4) + n0
            else:
                k = n0 // 1024
                c0 = 2 * OUTS + n0 % 1024
            return planes[4 * k : P, c0 : c0 + BANK]

        ipad = keep.tile([P, 2, 10, 10], BF16, name="ipad")
        ident4 = ident_bf[:].rearrange("p (b i j) -> p b i j", b=2, i=8)
        nc.vector.tensor_copy(out=ipad[:, :, 1:9, 1:9], in_=ident4)
        nc.vector.tensor_copy(out=ipad[:, :, 0, 1:9], in_=ident4[:, :, 1, :])
        nc.vector.tensor_copy(out=ipad[:, :, 9, 1:9], in_=ident4[:, :, 6, :])
        nc.vector.tensor_copy(out=ipad[:, :, :, 0], in_=ipad[:, :, :, 2])
        nc.vector.tensor_copy(out=ipad[:, :, :, 9], in_=ipad[:, :, :, 7])
        sel = keep.tile([P, TAPS, P], BF16, name="sel")
        for kh in range(3):
            for kw in range(3):
                nc.vector.tensor_copy(
                    out=sel[:, 3 * kh + kw, :].rearrange("p (b i j) -> p b i j", b=2, i=8),
                    in_=ipad[:, :, kh : kh + 8, kw : kw + 8],
                )

        at_ps = bank(7, [P, 4, P], BF16, "at_ps")
        for h in range(4):
            nc.tensor.transpose(at_ps[:, h, :], a_sb[:, h, :, :].rearrange("p b x -> p (b x)"), ident_bf[:])
        at_sb = keep.tile([P, CHANNELS], BF16, name="at_sb")
        nc.vector.tensor_copy(
            out=at_sb[:].rearrange("q (p h) -> q p h", h=4), in_=at_ps[:].rearrange("q h p -> q p h")
        )

        ptap = keep.tile([P, TAPS, CHANNELS], BF16, name="ptap")
        stats = keep.tile([P, TAPS, 6], F32, name="stats")
        for pair in range(5):
            taps = [tap for tap in (2 * pair, 2 * pair + 1) if tap < TAPS]
            pt = bank(pair, [P, 2, CHANNELS], BF16, "pt_%d" % pair)
            for i, tap in enumerate(taps):
                nc.tensor.matmul(pt[:, i, :], lhsT=sel[:, tap, :], rhs=at_sb[:], start=True, stop=True)
            for i, tap in enumerate(taps):
                nc.vector.bn_stats(out=stats[:, tap, :], in_=pt[:, i, :])
            nc.scalar.copy(out=ptap[:, taps[0] : taps[0] + len(taps), :], in_=pt[:, 0 : len(taps), :])
        mv = keep.tile([P, 2], F32, name="mv")
        nc.vector.bn_aggr(out=mv[:], in_=stats[:].rearrange("p t s -> p (t s)"))
        std = keep.tile([P, 1], F32, name="std")
        nc.scalar.activation(out=std[:], in_=mv[:, 1:2], func=ACT.Sqrt, scale=PATCH / (PATCH - 1.0))
        total = keep.tile([P, 1], F32, name="total")
        nc.vector.tensor_reduce(
            out=total[:],
            in_=stats[:].rearrange("p t (e s) -> p (t e) s", s=3)[:, :, 1],
            axis=mybir.AxisListType.X,
            op=ALU.add,
        )
        mean = keep.tile([P, 1], F32, name="mean")
        nc.vector.tensor_scalar(out=mean[:], in0=total[:], scalar1=1.0 / (2 * TAPS), scalar2=None, op0=ALU.mult)
        rstd = keep.tile([P, 1], F32, name="rstd")
        nc.vector.reciprocal(out=rstd[:], in_=std[:])
        nmr = keep.tile([P, 1], F32, name="nmr")
        nc.vector.tensor_scalar(
            out=nmr[:], in0=mean[:, 0:1], scalar1=rstd[:, 0:1], scalar2=-1.0, op0=ALU.mult, op1=ALU.mult
        )

        pn = keep.tile([P, PATCH], BF16, name="pn")
        grouped = keep.tile([P, PASSES, 4 * P], BF16, name="grouped", align_bytes=64)
        xc = keep.tile([P, PASSES, P], I32, name="xc", align_bytes=64)
        xs = keep.tile([P, PASSES, P], U8, name="xs", align_bytes=64)

        def normalise(j):
            dst = pn[:, 576 * j : 576 * (j + 1)].rearrange("p (c t) -> p c t", t=TAPS)
            src = ptap[:, :, 64 * j : 64 * (j + 1)].rearrange("p t c -> p c t")
            if j % 2 == 1:
                nc.scalar.activation(out=dst, in_=src, func=ACT.Identity, scale=rstd[:, 0:1], bias=nmr[:, 0:1])
            else:
                nc.vector.tensor_scalar(
                    out=dst, in0=src, scalar1=mean[:, 0:1], scalar2=rstd[:, 0:1], op0=ALU.subtract, op1=ALU.mult
                )

        def flip(g):
            xt = bank(4 + g % 4, [P, 4, P], BF16, "xt_%d" % g)
            for t in range(4):
                nc.tensor.transpose(xt[:, t, :], pn[:, 512 * g + t : 512 * (g + 1) : 4], ident_bf[:])
            dst = grouped[:, g, :].rearrange("p (r t) -> p r t", t=4)
            src = xt[:].rearrange("p t r -> p r t")
            if g % 3 == 2:
                nc.vector.tensor_copy(out=dst, in_=src)
            else:
                nc.scalar.copy(out=dst, in_=src)

        def quantise(g):
            nc.vector.quantize_mx(out=xc[:, g, :].bitcast(FP8X4), scales=xs[:, g, :], in_=grouped[:, g, :])

        acc = {}

        def passes(blk, g):
            for beta in range(4):
                if g == 0:
                    acc[(blk, beta)] = bank(4 * blk + beta, [P, BANK], F32, "acc_%d_%d" % (blk, beta))
                nc.tensor.matmul_mx(
                    out=acc[(blk, beta)][:],
                    lhsT=xc[:, g, :].bitcast(FP8X4),
                    lhsT_scale=xs[:, g, :],
                    rhs=w_piece[(blk, g, beta)].bitcast(FP8X4),
                    rhs_scale=plane_of(g, HALF * blk + BANK * beta),
                    start=(g == 0),
                    stop=(g == PASSES - 1),
                )

        def copy_on(which, dst, src):
            if which % 2 == 0:
                nc.vector.tensor_copy(out=dst, in_=src)
            else:
                nc.scalar.copy(out=dst, in_=src)

        def sort_out(banks, per, r_sb, first):
            width = BANK // per
            for i, bk in enumerate(banks):
                copy_on(
                    first + i,
                    r_sb[:, :, width * i : width * (i + 1)],
                    bk[:].rearrange("t (p j) -> t j p", j=per),
                )

        def flip_and_store(n0, per, r_sb, o_sb, first, label):
            for jj in range(per // 4):
                tp = bank((first + jj) % 4, [P, 4, P], F32, "tp_%s_%d" % (label, jj))
                for j in range(4):
                    nc.tensor.transpose(tp[:, j, :], r_sb[:, 4 * jj + j, :], ident_f[:])
                copy_on(
                    first + jj,
                    o_sb[:, :, 4 * jj : 4 * jj + 4, :],
                    tp[:].rearrange("p j (b x) -> p b j x", b=2),
                )
            nc.sync.dma_start(
                out=out[:, n0 : n0 + P * per].rearrange("b (p j) i x -> p b (j i x)", j=per),
                in_=o_sb[:].rearrange("p b j x -> p b (j x)"),
            )

        for step in range(PASSES + 2):
            if step < 8:
                normalise(step)
            if 1 <= step <= PASSES:
                flip(step - 1)
            if step >= 2:
                quantise(step - 2)
                passes(0, step - 2)
        r0 = keep.tile([P, 16, P], F32, name="r0")
        o0 = keep.tile([P, 2, 16, 64], F32, name="o0")
        sort_out([acc[(0, beta)] for beta in range(4)], 16, r0, 0)
        passes(1, 0)
        passes(1, 1)
        flip_and_store(0, 16, r0, o0, 0, "a")
        for g in range(2, PASSES):
            passes(1, g)
        r1 = []
        o1 = []
        for beta in range(4):
            r1.append(keep.tile([P, 4, P], F32, name="r1_%d" % beta))
            o1.append(keep.tile([P, 2, 4, 64], F32, name="o1_%d" % beta))
            sort_out([acc[(1, beta)]], 4, r1[beta], beta)
        for beta in range(4):
            flip_and_store(HALF + BANK * beta, 4, r1[beta], o1[beta], beta, "b%d" % beta)
